import numpy as np
import ml_dtypes


def mxq(x, axis, fmt="e4m3"):
    dtype, down = {"e4m3": (ml_dtypes.float8_e4m3fn, 7), "e5m2": (ml_dtypes.float8_e5m2, 14)}[fmt]
    v = np.moveaxis(np.asarray(x, np.float32).astype(ml_dtypes.bfloat16).astype(np.float64), axis, -1)
    blocks = v.reshape(v.shape[:-1] + (-1, 32))
    amax = np.abs(blocks).max(-1, keepdims=True)
    byte = np.maximum(np.where(amax > 0, np.frexp(amax)[1] - 1 + 127, 0) - down, 1)
    scale = np.exp2(byte - 127.0)
    codes = (blocks / scale).astype(np.float32).astype(dtype).astype(np.float64)
    return np.moveaxis((codes * scale).reshape(v.shape), -1, axis)


WIDE = False


def mx_kscale(k):
    if not WIDE:
        return np.ones(k)
    levels = np.array([10, -10, 5, -5, 0])
    if k % 512:
        return np.exp2(np.random.permutation(np.resize(levels, k // 32))).repeat(32)
    a = np.empty((k // 512, 16))
    for p in range(k // 512):
        a[p, :8] = np.random.permutation(np.resize(levels, 8))
        for g in range(8):
            far = levels[np.abs(levels - a[p, g]) >= 10]
            a[p, g + 8] = far[np.random.randint(len(far))]
    return np.exp2(a.ravel()).repeat(32)


BF16 = ml_dtypes.bfloat16


def bf(x):
    return np.asarray(x, np.float32).astype(BF16)


def f64(x):
    return np.asarray(x).astype(np.float64)


B, S, H, QD, KD, R = 4, 2048, 512, 128, 128, 128
SCALING = 2.0


def setup_inputs():
    s = mx_kscale(H)

    def w(o):
        return bf(np.random.standard_normal((o, H)) / np.sqrt(H) / s[None, :])

    def xa():
        return bf(np.random.standard_normal((B, S, R)) * 0.6)

    def up(o):
        return bf(np.random.standard_normal((R, o)) * 0.4 / np.sqrt(R))

    def bias(o):
        return bf(np.random.standard_normal(o) * 0.3)

    return {"x": bf(np.random.standard_normal((B, S, H)) * s),
            "Wq": w(QD), "Wk": w(KD), "Wv": w(KD),
            "bq": bias(QD), "bk": bias(KD), "bv": bias(KD),
            "xa_q": xa(), "xa_k": xa(), "xa_v": xa(),
            "Bq": up(QD), "Bk": up(KD), "Bv": up(KD)}


def lora_proj(xq, W, b, xa, Bm):
    base = xq @ mxq(f64(W), 1, "e4m3").T
    delta = f64(xa) @ f64(Bm)
    return base + SCALING * delta + f64(b)


def reference(x, Wq, Wk, Wv, bq, bk, bv, xa_q, xa_k, xa_v, Bq, Bk, Bv):
    xq = mxq(f64(x), 2, "e4m3")
    q = lora_proj(xq, Wq, bq, xa_q, Bq)
    k = lora_proj(xq, Wk, bk, xa_k, Bk)
    v = lora_proj(xq, Wv, bv, xa_v, Bv)
    return q, k, v

@@ -1,0 +1,348 @@
+from contextlib import ExitStack
+
+import concourse.mybir as mybir
+from concourse.masks import make_identity
+
+F32 = mybir.dt.float32
+BF16 = mybir.dt.bfloat16
+U32 = mybir.dt.uint32
+U8 = mybir.dt.uint8
+FP8X4 = mybir.dt.float8_e4m3fn_x4
+ADD = mybir.AluOpType.add
+MULT = mybir.AluOpType.mult
+
+P = 128
+TOKENS = 8192
+HID = 512
+OUT = 128
+RANK = 128
+KINDS = 3
+NT = TOKENS // P
+QUAD = 4
+NQ = NT // QUAD
+BANKS = 8
+SCALING = 2.0
+
+FLOPS = 2 * TOKENS * KINDS * OUT * (HID + RANK)
+
+X_CHUNKS = [4, 4, 8, 8, 8, 8, 8, 8, 8]
+XA_CHUNKS = [4, 4, 8, 16, 16, 16]
+LOAD_ORDER = [
+    ("xa", 0), ("w", 0), ("x", 0), ("up", 0), ("bias", 0), ("xa", 1), ("x", 1), ("xa", 2), ("x", 2), ("xa", 3), ("x", 3), ("x", 4), ("xa", 4), ("x", 5), ("x", 6), ("xa", 5), ("x", 7), ("x", 8),
+]
+RES_TILES = 8
+TAPER = 2
+
+
+def tile_loraqkvlinear_pa_t_kernel(
+    tc, x, Wq, Wk, Wv, bq, bk, bv, xa_q, xa_k, xa_v, Bq, Bk, Bv, out_0, out_1, out_2
+):
+    nc = tc.nc
+    xv = x.flatten_outer_dims().rearrange("(p j) h -> p j h", j=NT)
+    xav = [a.flatten_outer_dims().rearrange("(p j) r -> p j r", j=NT) for a in (xa_q, xa_k, xa_v)]
+    ov = [o.flatten_outer_dims().rearrange("(p j) o -> p j o", j=NT) for o in (out_0, out_1, out_2)]
+    ws = (Wq, Wk, Wv)
+    bs = (bq, bk, bv)
+    ups = (Bq, Bk, Bv)
+
+    with ExitStack() as ctx:
+        consts = ctx.enter_context(tc.tile_pool(name="consts", bufs=1))
+        inputs = ctx.enter_context(tc.tile_pool(name="inputs", bufs=1))
+        ring2 = ctx.enter_context(tc.tile_pool(name="ring2", bufs=2))
+        ring3 = ctx.enter_context(tc.tile_pool(name="ring3", bufs=3))
+        results = ctx.enter_context(tc.tile_pool(name="results", bufs=5))
+        psum = ctx.enter_context(tc.psum_pool(name="psum", bufs=1))
+        ctx.enter_context(tc.manual_schedule())
+
+        ident_f = consts.tile([P, P], F32, name="ident_f")
+        make_identity(nc, ident_f[:])
+        ident_b = consts.tile([P, P], BF16, name="ident_b")
+        make_identity(nc, ident_b[:])
+
+        up_sb = consts.tile([P, KINDS, OUT], BF16, name="up_sb")
+        bias_row = consts.tile([P, KINDS, OUT], BF16, name="bias_row")
+        nc.vector.memset(bias_row[:], 0.0)
+        ones = consts.tile([P, 4 * P], BF16, name="ones")
+        nc.vector.memset(ones[:], 1.0)
+
+        warm = consts.tile([P, 2], F32, name="warm")
+        nc.vector.memset(warm[:, 0:1], 0.0)
+        nc.scalar.mul(out=warm[:, 1:2], in_=warm[:, 0:1], mul=SCALING)
+
+        w_sb = inputs.tile([P, KINDS, HID], BF16, name="w_sb")
+        x_of = {}
+        xa_of = {}
+        x_tiles = []
+        j0 = 0
+        for c, n in enumerate(X_CHUNKS):
+            xc = inputs.tile([P, n, HID], BF16, name="x%d" % c)
+            x_tiles.append((xc, j0, n))
+            for i in range(n):
+                x_of[j0 + i] = (xc, i)
+            j0 += n
+        xa_tiles = []
+        j0 = 0
+        for c, n in enumerate(XA_CHUNKS):
+            group = []
+            for k in range(KINDS):
+                xac = inputs.tile([P, n, RANK], BF16, name="xa%d_%d" % (k, c))
+                group.append(xac)
+                for i in range(n):
+                    xa_of[(k, j0 + i)] = (xac, i)
+            xa_tiles.append((group, j0, n))
+            j0 += n
+        for what, c in LOAD_ORDER:
+            if what == "w":
+                for k in range(KINDS):
+                    nc.sync.dma_start(out=w_sb[:, k, :], in_=ws[k])
+            elif what == "up":
+                for k in range(KINDS):
+                    nc.sync.dma_start(out=up_sb[:, k, :], in_=ups[k])
+            elif what == "bias":
+                for k in range(KINDS):
+                    nc.sync.dma_start(out=bias_row[0:1, k, :], in_=bs[k].unsqueeze(0))
+            elif what == "x":
+                xc, j0, n = x_tiles[c]
+                nc.sync.dma_start(out=xc[:], in_=xv[:, j0 : j0 + n, :])
+            else:
+                group, j0, n = xa_tiles[c]
+                for k in range(KINDS):
+                    nc.sync.dma_start(out=group[k][:], in_=xav[k][:, j0 : j0 + n, :])
+
+        count = [0]
+
+        def bank(shape, dtype):
+            i = count[0] % BANKS
+            count[0] += 1
+            return psum.tile(shape, dtype, name="bank%d" % i, tag="bank%d" % i)
+
+        codes = {}
+        planes = {}
+        xaT = {}
+        tt = {}
+        mb = {}
+        res = {}
+
+        def valid(g):
+            return 0 <= g < NQ
+
+        def word_transposes(srcs):
+            xt = bank([P, 2, 2, P], F32)
+            for i, src in enumerate(srcs):
+                words = src.bitcast(F32)
+                for u in range(2):
+                    nc.tensor.transpose(xt[:, i, u, :], words[:, u : 2 * P : 2], ident_f[:])
+            return xt
+
+        def copy_words(grouped, first, n, xt):
+            view = grouped[:].bitcast(F32).rearrange("p (t r u) -> p t r u", r=P, u=2)
+            nc.scalar.copy(
+                out=view[:, first : first + n, :, :],
+                in_=xt[:, 0:n, :, :].rearrange("p t u r -> p t r u"),
+            )
+
+        w_grouped = consts.tile([P, KINDS * HID], BF16, name="w_grouped", align_bytes=64)
+        w_codes = consts.tile([P, KINDS * OUT], U32, name="w_codes", align_bytes=64)
+        w_planes = consts.tile([P, KINDS * OUT], U8, name="w_planes", align_bytes=64)
+        bias_f = consts.tile([P, 2, QUAD * OUT], F32, name="bias_f")
+
+        def weights_pe():
+            return [word_transposes([w_sb[:, 0, :], w_sb[:, 1, :]]), word_transposes([w_sb[:, 2, :]])]
+
+        def weights_rest(wt):
+            copy_words(w_grouped, 0, 2, wt[0])
+            copy_words(w_grouped, 2, 1, wt[1])
+            nc.vector.quantize_mx(
+                out=w_codes[:, 0 : 2 * OUT].bitcast(FP8X4),
+                scales=w_planes[:, 0 : 2 * OUT],
+                in_=w_grouped[:, 0 : 2 * HID],
+            )
+            nc.vector.quantize_mx(
+                out=w_codes[:, 2 * OUT : 3 * OUT].bitcast(FP8X4),
+                scales=w_planes[:, 2 * OUT : 3 * OUT],
+                in_=w_grouped[:, 2 * HID : 3 * HID],
+            )
+
+        def bias_pe():
+            pb = bank([P, KINDS, OUT], F32)
+            for k in range(KINDS):
+                nc.tensor.matmul(pb[:, k, :], lhsT=ones[:, 0:P], rhs=bias_row[:, k, :], start=True, stop=True)
+            return pb
+
+        def bias_rest(pb):
+            nc.vector.tensor_copy(
+                out=bias_f[:, 0, :].rearrange("p (i c) -> p i c", i=2),
+                in_=pb[:, 0:2, :].rearrange("p k o -> p (k o)").unsqueeze(1).to_broadcast([P, 2, 2 * OUT]),
+            )
+            nc.vector.tensor_copy(
+                out=bias_f[:, 1, :].rearrange("p (i o) -> p i o", i=QUAD),
+                in_=pb[:, 2, :].unsqueeze(1).to_broadcast([P, QUAD, OUT]),
+            )
+
+        def x_src(j):
+            xc, i = x_of[j]
+            return xc[:, i, :]
+
+        def tx_pe(g):
+            return [word_transposes([x_src(QUAD * g + 2 * h), x_src(QUAD * g + 2 * h + 1)]) for h in range(2)]
+
+        def txa_pe(g):
+            out = []
+            for h in range(2):
+                xat = bank([P, 6, P], BF16)
+                for s in range(6):
+                    k, i = divmod(6 * h + s, QUAD)
+                    xac, loc = xa_of[(k, QUAD * g + i)]
+                    nc.tensor.transpose(xat[:, s, :], xac[:, loc, :], ident_b[:])
+                out.append(xat)
+            return out
+
+        def delta_pe(g):
+            out = []
+            for h in range(2):
+                d = bank([P, 2, 2, OUT], F32)
+                for i in range(2):
+                    for k in range(2):
+                        nc.tensor.matmul(
+                            d[:, i, k, :],
+                            lhsT=xaT[g][:, QUAD * k + 2 * h + i, :],
+                            rhs=up_sb[:, k, :],
+                            start=True,
+                            stop=True,
+                        )
+                out.append(d)
+            d = bank([P, QUAD, OUT], F32)
+            for i in range(QUAD):
+                nc.tensor.matmul(d[:, i, :], lhsT=xaT[g][:, QUAD * 2 + i, :], rhs=up_sb[:, 2, :], start=True, stop=True)
+            out.append(d)
+            return out
+
+        def mx_pass(out, g, i, lo, hi):
+            nc.tensor.matmul_mx(
+                out=out,
+                lhsT=codes[g][:, i * P : (i + 1) * P].bitcast(FP8X4),
+                lhsT_scale=planes[g][:, i * P : (i + 1) * P],
+                rhs=w_codes[:, lo:hi].bitcast(FP8X4),
+                rhs_scale=w_planes[:, lo:hi],
+                start=True,
+                stop=True,
+            )
+
+        def base_pe(g):
+            for h in range(2):
+                m = bank([P, 2, 2 * OUT], F32)
+                for i in range(2):
+                    mx_pass(m[:, i, :], g, 2 * h + i, 0, 2 * OUT)
+                mb[(g, h)] = m
+            m = bank([P, QUAD, OUT], F32)
+            for i in range(QUAD):
+                mx_pass(m[:, i, :], g, i, 2 * OUT, 3 * OUT)
+            mb[(g, 2)] = m
+
+        def flat(ap):
+            if ap.ndim == 4:
+                return ap.rearrange("p a b c -> p (a b c)")
+            return ap.rearrange("p a b -> p (a b)")
+
+        def delta_out_vector(g, k, d):
+            t = ring3.tile([P, QUAD * OUT], F32, name="t%d" % k)
+            nc.vector.scalar_tensor_tensor(
+                out=t[:], in0=flat(d[:]), scalar=SCALING, in1=bias_f[:, k // 2, :], op0=MULT, op1=ADD
+            )
+            tt[(g, k)] = t
+
+        def delta_out_scalar(g, k, d):
+            t = ring3.tile([P, QUAD * OUT], F32, name="t%d" % k)
+            nc.scalar.mul(out=t[:], in_=flat(d[:]), mul=SCALING)
+            tt[(g, k)] = t
+
+        def bias_gpsimd(g, k):
+            t = tt[(g, k)]
+            nc.gpsimd.tensor_tensor(out=t[:], in0=t[:], in1=bias_f[:, k // 2, :], op=ADD)
+
+        def store(g, c, half, r, k):
+            if g >= NQ - TAPER:
+                j0 = g * QUAD
+                nc.sync.dma_start(out=ov[k][:, j0 : j0 + QUAD, :], in_=r[:, k, half * QUAD : (half + 1) * QUAD, :])
+            elif half == RES_TILES // QUAD - 1:
+                nc.sync.dma_start(out=ov[k][:, c * RES_TILES : (c + 1) * RES_TILES, :], in_=r[:, k, :, :])
+
+        def base_out(g, k):
+            c, half = divmod(g, RES_TILES // QUAD)
+            if c not in res:
+                res[c] = results.tile([P, KINDS, RES_TILES, OUT], F32, name="res")
+            r = res[c]
+            if k < 2:
+                j0 = half * QUAD + 2 * k
+                nc.vector.tensor_tensor(
+                    out=r[:, 0:2, j0 : j0 + 2, :].rearrange("p k i o -> p i k o"),
+                    in0=mb[(g, k)][:].rearrange("p i (k o) -> p i k o", k=2),
+                    in1=tt[(g, k)][:].rearrange("p (i k o) -> p i k o", i=2, k=2),
+                    op=ADD,
+                )
+                if k == 1:
+                    store(g, c, half, r, 0)
+                    store(g, c, half, r, 1)
+            else:
+                nc.vector.tensor_tensor(
+                    out=r[:, 2, half * QUAD : (half + 1) * QUAD, :],
+                    in0=mb[(g, k)][:],
+                    in1=tt[(g, k)][:].rearrange("p (i o) -> p i o", i=QUAD),
+                    op=ADD,
+                )
+                store(g, c, half, r, 2)
+
+        idle = bank([P, 4 * P], F32)
+
+        def warm(n):
+            for i in range(n):
+                nc.tensor.matmul(idle[:], lhsT=ones[:, 0:P], rhs=ones[:], start=True, stop=True)
+
+        warm(4)
+
+        for g in range(-2, NQ + 1):
+            if valid(g + 1):
+                xts = tx_pe(g + 1)
+            if g == -1:
+                warm(2)
+            if valid(g + 2):
+                xats = txa_pe(g + 2)
+            if g == -2:
+                warm(2)
+                wt = weights_pe()
+                warm(1)
+            if g == -1:
+                pb = bias_pe()
+            if valid(g - 1):
+                base_out(g - 1, 1)
+                base_out(g - 1, 2)
+            if valid(g + 1):
+                grouped = ring2.tile([P, QUAD * HID], BF16, name="grouped", align_bytes=64)
+                copy_words(grouped, 0, 2, xts[0])
+                copy_words(grouped, 2, 2, xts[1])
+            if valid(g + 2):
+                xa_t = ring2.tile([P, KINDS * QUAD, P], BF16, name="xa_t")
+                nc.scalar.copy(out=xa_t[:, 0:6, :].bitcast(F32), in_=xats[0][:].bitcast(F32))
+                nc.scalar.copy(out=xa_t[:, 6:12, :].bitcast(F32), in_=xats[1][:].bitcast(F32))
+                xaT[g + 2] = xa_t
+            if g == -2:
+                weights_rest(wt)
+            if g == -1:
+                bias_rest(pb)
+            if valid(g + 1):
+                ds = delta_pe(g + 1)
+                delta_out_vector(g + 1, 0, ds[0])
+                delta_out_scalar(g + 1, 1, ds[1])
+                cw = ring2.tile([P, QUAD * P], U32, name="cw", align_bytes=64)
+                pl = ring2.tile([P, QUAD * P], U8, name="pl", align_bytes=64)
+                nc.vector.quantize_mx(out=cw[:].bitcast(FP8X4), scales=pl[:], in_=grouped[:])
+                codes[g + 1] = cw
+                planes[g + 1] = pl
+                bias_gpsimd(g + 1, 1)
+                delta_out_scalar(g + 1, 2, ds[2])
+            if valid(g):
+                base_pe(g)
+            if valid(g + 1):
+                bias_gpsimd(g + 1, 2)
+            if valid(g):
+                base_out(g, 0)

@@ -301,25 +301,30 @@ def tile_loraqkvlinear_pa_t_kernel(
         warm(4)
 
         for g in range(-2, NQ + 1):
+            if valid(g - 1):
+                base_out(g - 1, 1)
+                base_out(g - 1, 2)
             if valid(g + 1):
                 xts = tx_pe(g + 1)
             if g == -1:
                 warm(2)
+            if valid(g + 1):
+                ds = delta_pe(g + 1)
             if valid(g + 2):
                 xats = txa_pe(g + 2)
             if g == -2:
                 warm(2)
                 wt = weights_pe()
                 warm(1)
-            if g == -1:
                 pb = bias_pe()
-            if valid(g - 1):
-                base_out(g - 1, 1)
-                base_out(g - 1, 2)
             if valid(g + 1):
                 grouped = ring2.tile([P, QUAD * HID], BF16, name="grouped", align_bytes=64)
                 copy_words(grouped, 0, 2, xts[0])
                 copy_words(grouped, 2, 2, xts[1])
+            if valid(g + 1):
+                delta_out_vector(g + 1, 0, ds[0])
+                delta_out_scalar(g + 1, 1, ds[1])
+                delta_out_scalar(g + 1, 2, ds[2])
             if valid(g + 2):
                 xa_t = ring2.tile([P, KINDS * QUAD, P], BF16, name="xa_t")
                 nc.scalar.copy(out=xa_t[:, 0:6, :].bitcast(F32), in_=xats[0][:].bitcast(F32))
@@ -327,19 +332,14 @@ def tile_loraqkvlinear_pa_t_kernel(
                 xaT[g + 2] = xa_t
             if g == -2:
                 weights_rest(wt)
-            if g == -1:
                 bias_rest(pb)
             if valid(g + 1):
-                ds = delta_pe(g + 1)
-                delta_out_vector(g + 1, 0, ds[0])
-                delta_out_scalar(g + 1, 1, ds[1])
                 cw = ring2.tile([P, QUAD * P], U32, name="cw", align_bytes=64)
                 pl = ring2.tile([P, QUAD * P], U8, name="pl", align_bytes=64)
                 nc.vector.quantize_mx(out=cw[:].bitcast(FP8X4), scales=pl[:], in_=grouped[:])
                 codes[g + 1] = cw
                 planes[g + 1] = pl
                 bias_gpsimd(g + 1, 1)
-                delta_out_scalar(g + 1, 2, ds[2])
             if valid(g):
                 base_pe(g)
             if valid(g + 1):

@@ -31,6 +31,7 @@ LOAD_ORDER = [
     ("xa", 0), ("w", 0), ("x", 0), ("up", 0), ("bias", 0), ("xa", 1), ("x", 1), ("xa", 2), ("x", 2), ("xa", 3), ("x", 3), ("x", 4), ("xa", 4), ("x", 5), ("x", 6), ("xa", 5), ("x", 7), ("x", 8),
 ]
 RES_TILES = 8
+GROUPS = [[g] for g in range(NQ)]
 TAPER = 2
 
 
@@ -49,8 +50,8 @@ def tile_loraqkvlinear_pa_t_kernel(
         consts = ctx.enter_context(tc.tile_pool(name="consts", bufs=1))
         inputs = ctx.enter_context(tc.tile_pool(name="inputs", bufs=1))
         ring2 = ctx.enter_context(tc.tile_pool(name="ring2", bufs=2))
-        ring3 = ctx.enter_context(tc.tile_pool(name="ring3", bufs=3))
-        results = ctx.enter_context(tc.tile_pool(name="results", bufs=5))
+        ring3 = ctx.enter_context(tc.tile_pool(name="ring3", bufs=4))
+        results = ctx.enter_context(tc.tile_pool(name="results", bufs=4))
         psum = ctx.enter_context(tc.psum_pool(name="psum", bufs=1))
         ctx.enter_context(tc.manual_schedule())
 
@@ -123,9 +124,6 @@ def tile_loraqkvlinear_pa_t_kernel(
         mb = {}
         res = {}
 
-        def valid(g):
-            return 0 <= g < NQ
-
         def word_transposes(srcs):
             xt = bank([P, 2, 2, P], F32)
             for i, src in enumerate(srcs):
@@ -144,7 +142,7 @@ def tile_loraqkvlinear_pa_t_kernel(
         w_grouped = consts.tile([P, KINDS * HID], BF16, name="w_grouped", align_bytes=64)
         w_codes = consts.tile([P, KINDS * OUT], U32, name="w_codes", align_bytes=64)
         w_planes = consts.tile([P, KINDS * OUT], U8, name="w_planes", align_bytes=64)
-        bias_f = consts.tile([P, 2, QUAD * OUT], F32, name="bias_f")
+        bias_f = consts.tile([P, KINDS, OUT], F32, name="bias_f")
 
         def weights_pe():
             return [word_transposes([w_sb[:, 0, :], w_sb[:, 1, :]]), word_transposes([w_sb[:, 2, :]])]
@@ -170,14 +168,15 @@ def tile_loraqkvlinear_pa_t_kernel(
             return pb
 
         def bias_rest(pb):
-            nc.vector.tensor_copy(
-                out=bias_f[:, 0, :].rearrange("p (i c) -> p i c", i=2),
-                in_=pb[:, 0:2, :].rearrange("p k o -> p (k o)").unsqueeze(1).to_broadcast([P, 2, 2 * OUT]),
-            )
-            nc.vector.tensor_copy(
-                out=bias_f[:, 1, :].rearrange("p (i o) -> p i o", i=QUAD),
-                in_=pb[:, 2, :].unsqueeze(1).to_broadcast([P, QUAD, OUT]),
-            )
+            nc.vector.tensor_copy(out=bias_f[:], in_=pb[:])
+
+        def bias_of(k):
+            if k < 2:
+                return bias_f[:, 0:2, :].rearrange("p k o -> p (k o)").unsqueeze(1).to_broadcast([P, 2, 2 * OUT])
+            return bias_f[:, 2, :].unsqueeze(1).to_broadcast([P, QUAD, OUT])
+
+        def split_cols(ap, k):
+            return ap.rearrange("p (i c) -> p i c", c=2 * OUT if k < 2 else OUT)
 
         def x_src(j):
             xc, i = x_of[j]
@@ -247,7 +246,7 @@ def tile_loraqkvlinear_pa_t_kernel(
         def delta_out_vector(g, k, d):
             t = ring3.tile([P, QUAD * OUT], F32, name="t%d" % k)
             nc.vector.scalar_tensor_tensor(
-                out=t[:], in0=flat(d[:]), scalar=SCALING, in1=bias_f[:, k // 2, :], op0=MULT, op1=ADD
+                out=split_cols(t[:], k), in0=split_cols(flat(d[:]), k), scalar=SCALING, in1=bias_of(k), op0=MULT, op1=ADD
             )
             tt[(g, k)] = t
 
@@ -258,7 +257,7 @@ def tile_loraqkvlinear_pa_t_kernel(
 
         def bias_gpsimd(g, k):
             t = tt[(g, k)]
-            nc.gpsimd.tensor_tensor(out=t[:], in0=t[:], in1=bias_f[:, k // 2, :], op=ADD)
+            nc.gpsimd.tensor_tensor(out=split_cols(t[:], k), in0=split_cols(t[:], k), in1=bias_of(k), op=ADD)
 
         def store(g, c, half, r, k):
             if g >= NQ - TAPER:
@@ -300,49 +299,42 @@ def tile_loraqkvlinear_pa_t_kernel(
 
         warm(4)
 
-        for g in range(-2, NQ + 1):
-            if valid(g - 1):
-                base_out(g - 1, 1)
-                base_out(g - 1, 2)
-            if valid(g + 1):
-                xts = tx_pe(g + 1)
-            if g == -1:
-                warm(2)
-            if valid(g + 1):
-                ds = delta_pe(g + 1)
-            if valid(g + 2):
-                xats = txa_pe(g + 2)
-            if g == -2:
-                warm(2)
-                wt = weights_pe()
-                warm(1)
-                pb = bias_pe()
-            if valid(g + 1):
-                grouped = ring2.tile([P, QUAD * HID], BF16, name="grouped", align_bytes=64)
-                copy_words(grouped, 0, 2, xts[0])
-                copy_words(grouped, 2, 2, xts[1])
-            if valid(g + 1):
-                delta_out_vector(g + 1, 0, ds[0])
-                delta_out_scalar(g + 1, 1, ds[1])
-                delta_out_scalar(g + 1, 2, ds[2])
-            if valid(g + 2):
-                xa_t = ring2.tile([P, KINDS * QUAD, P], BF16, name="xa_t")
+        def group(i):
+            return GROUPS[i] if 0 <= i < len(GROUPS) else []
+
+        for step in range(-2, len(GROUPS) + 1):
+            for g in group(step - 1):
+                for k in range(KINDS):
+                    base_out(g, k)
+            xts = [tx_pe(g) for g in group(step + 1)]
+            grouped = {}
+            for g, xts_g in zip(group(step + 1), xts):
+                grouped[g] = ring2.tile([P, QUAD * HID], BF16, name="grouped", bufs=3, align_bytes=64)
+                copy_words(grouped[g], 0, 2, xts_g[0])
+                copy_words(grouped[g], 2, 2, xts_g[1])
+            if step == -1:
+                bias_rest(bias_pe())
+            for g in group(step + 1):
+                ds = delta_pe(g)
+                delta_out_vector(g, 0, ds[0])
+                delta_out_scalar(g, 1, ds[1])
+                bias_gpsimd(g, 1)
+                delta_out_scalar(g, 2, ds[2])
+                bias_gpsimd(g, 2)
+            for g in group(step + 2):
+                xats = txa_pe(g)
+                xa_t = ring2.tile([P, KINDS * QUAD, P], BF16, name="xa_t", bufs=4)
                 nc.scalar.copy(out=xa_t[:, 0:6, :].bitcast(F32), in_=xats[0][:].bitcast(F32))
                 nc.scalar.copy(out=xa_t[:, 6:12, :].bitcast(F32), in_=xats[1][:].bitcast(F32))
-                xaT[g + 2] = xa_t
-            if g == -2:
+                xaT[g] = xa_t
+            if step == -2:
+                wt = weights_pe()
                 weights_rest(wt)
-                bias_rest(pb)
-            if valid(g + 1):
-                cw = ring2.tile([P, QUAD * P], U32, name="cw", align_bytes=64)
-                pl = ring2.tile([P, QUAD * P], U8, name="pl", align_bytes=64)
-                nc.vector.quantize_mx(out=cw[:].bitcast(FP8X4), scales=pl[:], in_=grouped[:])
-                codes[g + 1] = cw
-                planes[g + 1] = pl
-                bias_gpsimd(g + 1, 1)
-            if valid(g):
+            for g in group(step + 1):
+                cw = ring2.tile([P, QUAD * P], U32, name="cw", bufs=4, align_bytes=64)
+                pl = ring2.tile([P, QUAD * P], U8, name="pl", bufs=4, align_bytes=64)
+                nc.vector.quantize_mx(out=cw[:].bitcast(FP8X4), scales=pl[:], in_=grouped[g][:])
+                codes[g] = cw
+                planes[g] = pl
+            for g in group(step):
                 base_pe(g)
-            if valid(g + 1):
-                bias_gpsimd(g + 1, 2)
-            if valid(g):
-                base_out(g, 0)

@@ -31,7 +31,6 @@ LOAD_ORDER = [
     ("xa", 0), ("w", 0), ("x", 0), ("up", 0), ("bias", 0), ("xa", 1), ("x", 1), ("xa", 2), ("x", 2), ("xa", 3), ("x", 3), ("x", 4), ("xa", 4), ("x", 5), ("x", 6), ("xa", 5), ("x", 7), ("x", 8),
 ]
 RES_TILES = 8
-GROUPS = [[g] for g in range(NQ)]
 TAPER = 2
 
 
@@ -185,36 +184,30 @@ def tile_loraqkvlinear_pa_t_kernel(
         def tx_pe(g):
             return [word_transposes([x_src(QUAD * g + 2 * h), x_src(QUAD * g + 2 * h + 1)]) for h in range(2)]
 
-        def txa_pe(g):
-            out = []
-            for h in range(2):
-                xat = bank([P, 6, P], BF16)
-                for s in range(6):
-                    k, i = divmod(6 * h + s, QUAD)
-                    xac, loc = xa_of[(k, QUAD * g + i)]
-                    nc.tensor.transpose(xat[:, s, :], xac[:, loc, :], ident_b[:])
-                out.append(xat)
-            return out
-
-        def delta_pe(g):
-            out = []
-            for h in range(2):
-                d = bank([P, 2, 2, OUT], F32)
-                for i in range(2):
-                    for k in range(2):
-                        nc.tensor.matmul(
-                            d[:, i, k, :],
-                            lhsT=xaT[g][:, QUAD * k + 2 * h + i, :],
-                            rhs=up_sb[:, k, :],
-                            start=True,
-                            stop=True,
-                        )
-                out.append(d)
-            d = bank([P, QUAD, OUT], F32)
-            for i in range(QUAD):
-                nc.tensor.matmul(d[:, i, :], lhsT=xaT[g][:, QUAD * 2 + i, :], rhs=up_sb[:, 2, :], start=True, stop=True)
-            out.append(d)
-            return out
+        def txa_delta_pe(gx, gd):
+            xats = []
+            ds = []
+            for n in range(KINDS * QUAD):
+                if gx is not None:
+                    if n % 6 == 0:
+                        xats.append(bank([P, 6, P], BF16))
+                    k, i = divmod(n, QUAD)
+                    xac, loc = xa_of[(k, QUAD * gx + i)]
+                    nc.tensor.transpose(xats[-1][:, n % 6, :], xac[:, loc, :], ident_b[:])
+                if gd is not None:
+                    b, c = divmod(n, QUAD)
+                    if c == 0:
+                        ds.append(bank([P, 2, 2, OUT] if b < 2 else [P, QUAD, OUT], F32))
+                    if b < 2:
+                        i, k = divmod(c, 2)
+                        out = ds[b][:, i, k, :]
+                        src = QUAD * k + 2 * b + i
+                    else:
+                        k = 2
+                        out = ds[b][:, c, :]
+                        src = QUAD * k + c
+                    nc.tensor.matmul(out, lhsT=xaT[gd][:, src, :], rhs=up_sb[:, k, :], start=True, stop=True)
+            return xats, ds
 
         def mx_pass(out, g, i, lo, hi):
             nc.tensor.matmul_mx(
@@ -299,42 +292,43 @@ def tile_loraqkvlinear_pa_t_kernel(
 
         warm(4)
 
-        def group(i):
-            return GROUPS[i] if 0 <= i < len(GROUPS) else []
+        def quad(g):
+            return g if 0 <= g < NQ else None
 
-        for step in range(-2, len(GROUPS) + 1):
-            for g in group(step - 1):
+        for g in range(-2, NQ + 1):
+            if quad(g - 1) is not None:
                 for k in range(KINDS):
-                    base_out(g, k)
-            xts = [tx_pe(g) for g in group(step + 1)]
-            grouped = {}
-            for g, xts_g in zip(group(step + 1), xts):
-                grouped[g] = ring2.tile([P, QUAD * HID], BF16, name="grouped", bufs=3, align_bytes=64)
-                copy_words(grouped[g], 0, 2, xts_g[0])
-                copy_words(grouped[g], 2, 2, xts_g[1])
-            if step == -1:
+                    base_out(g - 1, k)
+            if quad(g + 1) is not None:
+                xts = tx_pe(g + 1)
+                grouped = ring2.tile([P, QUAD * HID], BF16, name="grouped", bufs=3, align_bytes=64)
+                copy_words(grouped, 0, 2, xts[0])
+                copy_words(grouped, 2, 2, xts[1])
+            if g == -1:
                 bias_rest(bias_pe())
-            for g in group(step + 1):
-                ds = delta_pe(g)
-                delta_out_vector(g, 0, ds[0])
-                delta_out_scalar(g, 1, ds[1])
-                bias_gpsimd(g, 1)
-                delta_out_scalar(g, 2, ds[2])
-                bias_gpsimd(g, 2)
-            for g in group(step + 2):
-                xats = txa_pe(g)
+            xats, ds = txa_delta_pe(quad(g + 2), quad(g + 1))
+            if ds:
+                delta_out_vector(g + 1, 0, ds[0])
+            if xats:
                 xa_t = ring2.tile([P, KINDS * QUAD, P], BF16, name="xa_t", bufs=4)
                 nc.scalar.copy(out=xa_t[:, 0:6, :].bitcast(F32), in_=xats[0][:].bitcast(F32))
+                xaT[g + 2] = xa_t
+            if ds:
+                delta_out_scalar(g + 1, 1, ds[1])
+                bias_gpsimd(g + 1, 1)
+            if xats:
                 nc.scalar.copy(out=xa_t[:, 6:12, :].bitcast(F32), in_=xats[1][:].bitcast(F32))
-                xaT[g] = xa_t
-            if step == -2:
+            if ds:
+                delta_out_scalar(g + 1, 2, ds[2])
+                bias_gpsimd(g + 1, 2)
+            if g == -2:
                 wt = weights_pe()
                 weights_rest(wt)
-            for g in group(step + 1):
+            if quad(g + 1) is not None:
                 cw = ring2.tile([P, QUAD * P], U32, name="cw", bufs=4, align_bytes=64)
                 pl = ring2.tile([P, QUAD * P], U8, name="pl", bufs=4, align_bytes=64)
-                nc.vector.quantize_mx(out=cw[:].bitcast(FP8X4), scales=pl[:], in_=grouped[g][:])
-                codes[g] = cw
-                planes[g] = pl
-            for g in group(step):
+                nc.vector.quantize_mx(out=cw[:].bitcast(FP8X4), scales=pl[:], in_=grouped[:])
+                codes[g + 1] = cw
+                planes[g + 1] = pl
+            if quad(g) is not None:
                 base_pe(g)

@@ -50,7 +50,7 @@ def tile_loraqkvlinear_pa_t_kernel(
         inputs = ctx.enter_context(tc.tile_pool(name="inputs", bufs=1))
         ring2 = ctx.enter_context(tc.tile_pool(name="ring2", bufs=2))
         ring3 = ctx.enter_context(tc.tile_pool(name="ring3", bufs=4))
-        results = ctx.enter_context(tc.tile_pool(name="results", bufs=4))
+        results = ctx.enter_context(tc.tile_pool(name="results", bufs=5))
         psum = ctx.enter_context(tc.psum_pool(name="psum", bufs=1))
         ctx.enter_context(tc.manual_schedule())
 
@@ -188,12 +188,6 @@ def tile_loraqkvlinear_pa_t_kernel(
             xats = []
             ds = []
             for n in range(KINDS * QUAD):
-                if gx is not None:
-                    if n % 6 == 0:
-                        xats.append(bank([P, 6, P], BF16))
-                    k, i = divmod(n, QUAD)
-                    xac, loc = xa_of[(k, QUAD * gx + i)]
-                    nc.tensor.transpose(xats[-1][:, n % 6, :], xac[:, loc, :], ident_b[:])
                 if gd is not None:
                     b, c = divmod(n, QUAD)
                     if c == 0:
@@ -207,6 +201,12 @@ def tile_loraqkvlinear_pa_t_kernel(
                         out = ds[b][:, c, :]
                         src = QUAD * k + c
                     nc.tensor.matmul(out, lhsT=xaT[gd][:, src, :], rhs=up_sb[:, k, :], start=True, stop=True)
+                if gx is not None:
+                    if n % 6 == 0:
+                        xats.append(bank([P, 6, P], BF16))
+                    k, i = divmod(n, QUAD)
+                    xac, loc = xa_of[(k, QUAD * gx + i)]
+                    nc.tensor.transpose(xats[-1][:, n % 6, :], xac[:, loc, :], ident_b[:])
             return xats, ds
 
         def mx_pass(out, g, i, lo, hi):
@@ -310,7 +310,7 @@ def tile_loraqkvlinear_pa_t_kernel(
             if ds:
                 delta_out_vector(g + 1, 0, ds[0])
             if xats:
-                xa_t = ring2.tile([P, KINDS * QUAD, P], BF16, name="xa_t", bufs=4)
+                xa_t = ring2.tile([P, KINDS * QUAD, P], BF16, name="xa_t", bufs=3)
                 nc.scalar.copy(out=xa_t[:, 0:6, :].bitcast(F32), in_=xats[0][:].bitcast(F32))
                 xaT[g + 2] = xa_t
             if ds:
@@ -325,8 +325,8 @@ def tile_loraqkvlinear_pa_t_kernel(
                 wt = weights_pe()
                 weights_rest(wt)
             if quad(g + 1) is not None:
-                cw = ring2.tile([P, QUAD * P], U32, name="cw", bufs=4, align_bytes=64)
-                pl = ring2.tile([P, QUAD * P], U8, name="pl", bufs=4, align_bytes=64)
+                cw = ring2.tile([P, QUAD * P], U32, name="cw", bufs=3, align_bytes=64)
+                pl = ring2.tile([P, QUAD * P], U8, name="pl", bufs=3, align_bytes=64)
                 nc.vector.quantize_mx(out=cw[:].bitcast(FP8X4), scales=pl[:], in_=grouped[:])
                 codes[g + 1] = cw
                 planes[g + 1] = pl

@@ -25,10 +25,10 @@ SCALING = 2.0
 
 FLOPS = 2 * TOKENS * KINDS * OUT * (HID + RANK)
 
-X_CHUNKS = [4, 4, 8, 8, 8, 8, 8, 8, 8]
+X_CHUNKS = [4, 4, 4, 4, 8, 8, 8, 8, 8, 8]
 XA_CHUNKS = [4, 4, 8, 16, 16, 16]
 LOAD_ORDER = [
-    ("xa", 0), ("w", 0), ("x", 0), ("up", 0), ("bias", 0), ("xa", 1), ("x", 1), ("xa", 2), ("x", 2), ("xa", 3), ("x", 3), ("x", 4), ("xa", 4), ("x", 5), ("x", 6), ("xa", 5), ("x", 7), ("x", 8),
+    ("xa", 0), ("w", 0), ("x", 0), ("up", 0), ("bias", 0), ("xa", 1), ("x", 1), ("xa", 2), ("x", 2), ("x", 3), ("xa", 3), ("x", 4), ("x", 5), ("xa", 4), ("x", 6), ("x", 7), ("xa", 5), ("x", 8), ("x", 9),
 ]
 RES_TILES = 8
 TAPER = 2
@@ -314,8 +314,11 @@ def tile_loraqkvlinear_pa_t_kernel(
                 nc.scalar.copy(out=xa_t[:, 0:6, :].bitcast(F32), in_=xats[0][:].bitcast(F32))
                 xaT[g + 2] = xa_t
             if ds:
-                delta_out_scalar(g + 1, 1, ds[1])
-                bias_gpsimd(g + 1, 1)
+                if g % 2 == 0:
+                    delta_out_vector(g + 1, 1, ds[1])
+                else:
+                    delta_out_scalar(g + 1, 1, ds[1])
+                    bias_gpsimd(g + 1, 1)
             if xats:
                 nc.scalar.copy(out=xa_t[:, 6:12, :].bitcast(F32), in_=xats[1][:].bitcast(F32))
             if ds:

@@ -28,10 +28,10 @@ FLOPS = 2 * TOKENS * KINDS * OUT * (HID + RANK)
 X_CHUNKS = [4, 4, 4, 4, 8, 8, 8, 8, 8, 8]
 XA_CHUNKS = [4, 4, 8, 16, 16, 16]
 LOAD_ORDER = [
-    ("xa", 0), ("w", 0), ("x", 0), ("up", 0), ("bias", 0), ("xa", 1), ("x", 1), ("xa", 2), ("x", 2), ("x", 3), ("xa", 3), ("x", 4), ("x", 5), ("xa", 4), ("x", 6), ("x", 7), ("xa", 5), ("x", 8), ("x", 9),
+    ("xa", 0), ("w", 0), ("x", 0), ("up", 0), ("xa", 1), ("bias", 0), ("x", 1), ("xa", 2), ("x", 2), ("x", 3), ("xa", 3), ("x", 4), ("x", 5), ("xa", 4), ("x", 6), ("x", 7), ("xa", 5), ("x", 8), ("x", 9),
 ]
 RES_TILES = 8
-TAPER = 2
+TAPER = 4
 
 
 def tile_loraqkvlinear_pa_t_kernel(
@@ -272,7 +272,11 @@ def tile_loraqkvlinear_pa_t_kernel(
                     in1=tt[(g, k)][:].rearrange("p (i k o) -> p i k o", i=2, k=2),
                     op=ADD,
                 )
-                if k == 1:
+                if g >= NQ - 2:
+                    t0 = g * QUAD + 2 * k
+                    for kind in range(2):
+                        nc.sync.dma_start(out=ov[kind][:, t0 : t0 + 2, :], in_=r[:, kind, j0 : j0 + 2, :])
+                elif k == 1:
                     store(g, c, half, r, 0)
                     store(g, c, half, r, 1)
             else:
@@ -299,14 +303,16 @@ def tile_loraqkvlinear_pa_t_kernel(
             if quad(g - 1) is not None:
                 for k in range(KINDS):
                     base_out(g - 1, k)
+            if g == -1:
+                warm(2)
             if quad(g + 1) is not None:
                 xts = tx_pe(g + 1)
                 grouped = ring2.tile([P, QUAD * HID], BF16, name="grouped", bufs=3, align_bytes=64)
                 copy_words(grouped, 0, 2, xts[0])
                 copy_words(grouped, 2, 2, xts[1])
+            xats, ds = txa_delta_pe(quad(g + 2), quad(g + 1))
             if g == -1:
                 bias_rest(bias_pe())
-            xats, ds = txa_delta_pe(quad(g + 2), quad(g + 1))
             if ds:
                 delta_out_vector(g + 1, 0, ds[0])
             if xats:
@@ -314,7 +320,7 @@ def tile_loraqkvlinear_pa_t_kernel(
                 nc.scalar.copy(out=xa_t[:, 0:6, :].bitcast(F32), in_=xats[0][:].bitcast(F32))
                 xaT[g + 2] = xa_t
             if ds:
-                if g % 2 == 0:
+                if g % 3 != 2 and g < NQ - 2:
                     delta_out_vector(g + 1, 1, ds[1])
                 else:
                     delta_out_scalar(g + 1, 1, ds[1])

from contextlib import ExitStack

import concourse.mybir as mybir
from concourse.masks import make_identity

F32 = mybir.dt.float32
BF16 = mybir.dt.bfloat16
U32 = mybir.dt.uint32
U8 = mybir.dt.uint8
FP8X4 = mybir.dt.float8_e4m3fn_x4
ADD = mybir.AluOpType.add
MULT = mybir.AluOpType.mult

P = 128
TOKENS = 8192
HID = 512
OUT = 128
RANK = 128
KINDS = 3
NT = TOKENS // P
QUAD = 4
NQ = NT // QUAD
BANKS = 8
SCALING = 2.0

FLOPS = 2 * TOKENS * KINDS * OUT * (HID + RANK)

X_CHUNKS = [4, 4, 4, 4, 8, 8, 8, 8, 8, 8]
XA_CHUNKS = [4, 4, 8, 16, 16, 16]
LOAD_ORDER = [
    ("xa", 0), ("w", 0), ("x", 0), ("up", 0), ("xa", 1), ("bias", 0), ("x", 1), ("xa", 2), ("x", 2), ("x", 3), ("xa", 3), ("x", 4), ("x", 5), ("xa", 4), ("x", 6), ("x", 7), ("xa", 5), ("x", 8), ("x", 9),
]
RES_TILES = 8
TAPER = 4


def tile_loraqkvlinear_pa_t_kernel(
    tc, x, Wq, Wk, Wv, bq, bk, bv, xa_q, xa_k, xa_v, Bq, Bk, Bv, out_0, out_1, out_2
):
    nc = tc.nc
    xv = x.flatten_outer_dims().rearrange("(p j) h -> p j h", j=NT)
    xav = [a.flatten_outer_dims().rearrange("(p j) r -> p j r", j=NT) for a in (xa_q, xa_k, xa_v)]
    ov = [o.flatten_outer_dims().rearrange("(p j) o -> p j o", j=NT) for o in (out_0, out_1, out_2)]
    ws = (Wq, Wk, Wv)
    bs = (bq, bk, bv)
    ups = (Bq, Bk, Bv)

    with ExitStack() as ctx:
        consts = ctx.enter_context(tc.tile_pool(name="consts", bufs=1))
        inputs = ctx.enter_context(tc.tile_pool(name="inputs", bufs=1))
        ring2 = ctx.enter_context(tc.tile_pool(name="ring2", bufs=2))
        ring3 = ctx.enter_context(tc.tile_pool(name="ring3", bufs=4))
        results = ctx.enter_context(tc.tile_pool(name="results", bufs=5))
        psum = ctx.enter_context(tc.psum_pool(name="psum", bufs=1))
        ctx.enter_context(tc.manual_schedule())

        ident_f = consts.tile([P, P], F32, name="ident_f")
        make_identity(nc, ident_f[:])
        ident_b = consts.tile([P, P], BF16, name="ident_b")
        make_identity(nc, ident_b[:])

        up_sb = consts.tile([P, KINDS, OUT], BF16, name="up_sb")
        bias_row = consts.tile([P, KINDS, OUT], BF16, name="bias_row")
        nc.vector.memset(bias_row[:], 0.0)
        ones = consts.tile([P, 4 * P], BF16, name="ones")
        nc.vector.memset(ones[:], 1.0)

        warm = consts.tile([P, 2], F32, name="warm")
        nc.vector.memset(warm[:, 0:1], 0.0)
        nc.scalar.mul(out=warm[:, 1:2], in_=warm[:, 0:1], mul=SCALING)

        w_sb = inputs.tile([P, KINDS, HID], BF16, name="w_sb")
        x_of = {}
        xa_of = {}
        x_tiles = []
        j0 = 0
        for c, n in enumerate(X_CHUNKS):
            xc = inputs.tile([P, n, HID], BF16, name="x%d" % c)
            x_tiles.append((xc, j0, n))
            for i in range(n):
                x_of[j0 + i] = (xc, i)
            j0 += n
        xa_tiles = []
        j0 = 0
        for c, n in enumerate(XA_CHUNKS):
            group = []
            for k in range(KINDS):
                xac = inputs.tile([P, n, RANK], BF16, name="xa%d_%d" % (k, c))
                group.append(xac)
                for i in range(n):
                    xa_of[(k, j0 + i)] = (xac, i)
            xa_tiles.append((group, j0, n))
            j0 += n
        for what, c in LOAD_ORDER:
            if what == "w":
                for k in range(KINDS):
                    nc.sync.dma_start(out=w_sb[:, k, :], in_=ws[k])
            elif what == "up":
                for k in range(KINDS):
                    nc.sync.dma_start(out=up_sb[:, k, :], in_=ups[k])
            elif what == "bias":
                for k in range(KINDS):
                    nc.sync.dma_start(out=bias_row[0:1, k, :], in_=bs[k].unsqueeze(0))
            elif what == "x":
                xc, j0, n = x_tiles[c]
                nc.sync.dma_start(out=xc[:], in_=xv[:, j0 : j0 + n, :])
            else:
                group, j0, n = xa_tiles[c]
                for k in range(KINDS):
                    nc.sync.dma_start(out=group[k][:], in_=xav[k][:, j0 : j0 + n, :])

        count = [0]

        def bank(shape, dtype):
            i = count[0] % BANKS
            count[0] += 1
            return psum.tile(shape, dtype, name="bank%d" % i, tag="bank%d" % i)

        codes = {}
        planes = {}
        xaT = {}
        tt = {}
        mb = {}
        res = {}

        def word_transposes(srcs):
            xt = bank([P, 2, 2, P], F32)
            for i, src in enumerate(srcs):
                words = src.bitcast(F32)
                for u in range(2):
                    nc.tensor.transpose(xt[:, i, u, :], words[:, u : 2 * P : 2], ident_f[:])
            return xt

        def copy_words(grouped, first, n, xt):
            view = grouped[:].bitcast(F32).rearrange("p (t r u) -> p t r u", r=P, u=2)
            nc.scalar.copy(
                out=view[:, first : first + n, :, :],
                in_=xt[:, 0:n, :, :].rearrange("p t u r -> p t r u"),
            )

        w_grouped = consts.tile([P, KINDS * HID], BF16, name="w_grouped", align_bytes=64)
        w_codes = consts.tile([P, KINDS * OUT], U32, name="w_codes", align_bytes=64)
        w_planes = consts.tile([P, KINDS * OUT], U8, name="w_planes", align_bytes=64)
        bias_f = consts.tile([P, KINDS, OUT], F32, name="bias_f")

        def weights_pe():
            return [word_transposes([w_sb[:, 0, :], w_sb[:, 1, :]]), word_transposes([w_sb[:, 2, :]])]

        def weights_rest(wt):
            copy_words(w_grouped, 0, 2, wt[0])
            copy_words(w_grouped, 2, 1, wt[1])
            nc.vector.quantize_mx(
                out=w_codes[:, 0 : 2 * OUT].bitcast(FP8X4),
                scales=w_planes[:, 0 : 2 * OUT],
                in_=w_grouped[:, 0 : 2 * HID],
            )
            nc.vector.quantize_mx(
                out=w_codes[:, 2 * OUT : 3 * OUT].bitcast(FP8X4),
                scales=w_planes[:, 2 * OUT : 3 * OUT],
                in_=w_grouped[:, 2 * HID : 3 * HID],
            )

        def bias_pe():
            pb = bank([P, KINDS, OUT], F32)
            for k in range(KINDS):
                nc.tensor.matmul(pb[:, k, :], lhsT=ones[:, 0:P], rhs=bias_row[:, k, :], start=True, stop=True)
            return pb

        def bias_rest(pb):
            nc.vector.tensor_copy(out=bias_f[:], in_=pb[:])

        def bias_of(k):
            if k < 2:
                return bias_f[:, 0:2, :].rearrange("p k o -> p (k o)").unsqueeze(1).to_broadcast([P, 2, 2 * OUT])
            return bias_f[:, 2, :].unsqueeze(1).to_broadcast([P, QUAD, OUT])

        def split_cols(ap, k):
            return ap.rearrange("p (i c) -> p i c", c=2 * OUT if k < 2 else OUT)

        def x_src(j):
            xc, i = x_of[j]
            return xc[:, i, :]

        def tx_pe(g):
            return [word_transposes([x_src(QUAD * g + 2 * h), x_src(QUAD * g + 2 * h + 1)]) for h in range(2)]

        def txa_delta_pe(gx, gd):
            xats = []
            ds = []
            for n in range(KINDS * QUAD):
                if gd is not None:
                    b, c = divmod(n, QUAD)
                    if c == 0:
                        ds.append(bank([P, 2, 2, OUT] if b < 2 else [P, QUAD, OUT], F32))
                    if b < 2:
                        i, k = divmod(c, 2)
                        out = ds[b][:, i, k, :]
                        src = QUAD * k + 2 * b + i
                    else:
                        k = 2
                        out = ds[b][:, c, :]
                        src = QUAD * k + c
                    nc.tensor.matmul(out, lhsT=xaT[gd][:, src, :], rhs=up_sb[:, k, :], start=True, stop=True)
                if gx is not None:
                    if n % 6 == 0:
                        xats.append(bank([P, 6, P], BF16))
                    k, i = divmod(n, QUAD)
                    xac, loc = xa_of[(k, QUAD * gx + i)]
                    nc.tensor.transpose(xats[-1][:, n % 6, :], xac[:, loc, :], ident_b[:])
            return xats, ds

        def mx_pass(out, g, i, lo, hi):
            nc.tensor.matmul_mx(
                out=out,
                lhsT=codes[g][:, i * P : (i + 1) * P].bitcast(FP8X4),
                lhsT_scale=planes[g][:, i * P : (i + 1) * P],
                rhs=w_codes[:, lo:hi].bitcast(FP8X4),
                rhs_scale=w_planes[:, lo:hi],
                start=True,
                stop=True,
            )

        def base_pe(g):
            for h in range(2):
                m = bank([P, 2, 2 * OUT], F32)
                for i in range(2):
                    mx_pass(m[:, i, :], g, 2 * h + i, 0, 2 * OUT)
                mb[(g, h)] = m
            m = bank([P, QUAD, OUT], F32)
            for i in range(QUAD):
                mx_pass(m[:, i, :], g, i, 2 * OUT, 3 * OUT)
            mb[(g, 2)] = m

        def flat(ap):
            if ap.ndim == 4:
                return ap.rearrange("p a b c -> p (a b c)")
            return ap.rearrange("p a b -> p (a b)")

        def delta_out_vector(g, k, d):
            t = ring3.tile([P, QUAD * OUT], F32, name="t%d" % k)
            nc.vector.scalar_tensor_tensor(
                out=split_cols(t[:], k), in0=split_cols(flat(d[:]), k), scalar=SCALING, in1=bias_of(k), op0=MULT, op1=ADD
            )
            tt[(g, k)] = t

        def delta_out_scalar(g, k, d):
            t = ring3.tile([P, QUAD * OUT], F32, name="t%d" % k)
            nc.scalar.mul(out=t[:], in_=flat(d[:]), mul=SCALING)
            tt[(g, k)] = t

        def bias_gpsimd(g, k):
            t = tt[(g, k)]
            nc.gpsimd.tensor_tensor(out=split_cols(t[:], k), in0=split_cols(t[:], k), in1=bias_of(k), op=ADD)

        def store(g, c, half, r, k):
            if g >= NQ - TAPER:
                j0 = g * QUAD
                nc.sync.dma_start(out=ov[k][:, j0 : j0 + QUAD, :], in_=r[:, k, half * QUAD : (half + 1) * QUAD, :])
            elif half == RES_TILES // QUAD - 1:
                nc.sync.dma_start(out=ov[k][:, c * RES_TILES : (c + 1) * RES_TILES, :], in_=r[:, k, :, :])

        def base_out(g, k):
            c, half = divmod(g, RES_TILES // QUAD)
            if c not in res:
                res[c] = results.tile([P, KINDS, RES_TILES, OUT], F32, name="res")
            r = res[c]
            if k < 2:
                j0 = half * QUAD + 2 * k
                nc.vector.tensor_tensor(
                    out=r[:, 0:2, j0 : j0 + 2, :].rearrange("p k i o -> p i k o"),
                    in0=mb[(g, k)][:].rearrange("p i (k o) -> p i k o", k=2),
                    in1=tt[(g, k)][:].rearrange("p (i k o) -> p i k o", i=2, k=2),
                    op=ADD,
                )
                if g >= NQ - 2:
                    t0 = g * QUAD + 2 * k
                    for kind in range(2):
                        nc.sync.dma_start(out=ov[kind][:, t0 : t0 + 2, :], in_=r[:, kind, j0 : j0 + 2, :])
                elif k == 1:
                    store(g, c, half, r, 0)
                    store(g, c, half, r, 1)
            else:
                nc.vector.tensor_tensor(
                    out=r[:, 2, half * QUAD : (half + 1) * QUAD, :],
                    in0=mb[(g, k)][:],
                    in1=tt[(g, k)][:].rearrange("p (i o) -> p i o", i=QUAD),
                    op=ADD,
                )
                store(g, c, half, r, 2)

        idle = bank([P, 4 * P], F32)

        def warm(n):
            for i in range(n):
                nc.tensor.matmul(idle[:], lhsT=ones[:, 0:P], rhs=ones[:], start=True, stop=True)

        warm(4)

        def quad(g):
            return g if 0 <= g < NQ else None

        for g in range(-2, NQ + 1):
            if quad(g - 1) is not None:
                for k in range(KINDS):
                    base_out(g - 1, k)
            if g == -1:
                warm(2)
            if quad(g + 1) is not None:
                xts = tx_pe(g + 1)
                grouped = ring2.tile([P, QUAD * HID], BF16, name="grouped", bufs=3, align_bytes=64)
                copy_words(grouped, 0, 2, xts[0])
                copy_words(grouped, 2, 2, xts[1])
            xats, ds = txa_delta_pe(quad(g + 2), quad(g + 1))
            if g == -1:
                bias_rest(bias_pe())
            if ds:
                delta_out_vector(g + 1, 0, ds[0])
            if xats:
                xa_t = ring2.tile([P, KINDS * QUAD, P], BF16, name="xa_t", bufs=3)
                nc.scalar.copy(out=xa_t[:, 0:6, :].bitcast(F32), in_=xats[0][:].bitcast(F32))
                xaT[g + 2] = xa_t
            if ds:
                if g % 3 != 2 and g < NQ - 2:
                    delta_out_vector(g + 1, 1, ds[1])
                else:
                    delta_out_scalar(g + 1, 1, ds[1])
                    bias_gpsimd(g + 1, 1)
            if xats:
                nc.scalar.copy(out=xa_t[:, 6:12, :].bitcast(F32), in_=xats[1][:].bitcast(F32))
            if ds:
                delta_out_scalar(g + 1, 2, ds[2])
                bias_gpsimd(g + 1, 2)
            if g == -2:
                wt = weights_pe()
                weights_rest(wt)
            if quad(g + 1) is not None:
                cw = ring2.tile([P, QUAD * P], U32, name="cw", bufs=3, align_bytes=64)
                pl = ring2.tile([P, QUAD * P], U8, name="pl", bufs=3, align_bytes=64)
                nc.vector.quantize_mx(out=cw[:].bitcast(FP8X4), scales=pl[:], in_=grouped[:])
                codes[g + 1] = cw
                planes[g + 1] = pl
            if quad(g) is not None:
                base_pe(g)
